import numpy as np
import ml_dtypes


def mxq(x, axis, fmt="e4m3"):
    dtype, down = {"e4m3": (ml_dtypes.float8_e4m3fn, 7), "e5m2": (ml_dtypes.float8_e5m2, 14)}[fmt]
    v = np.moveaxis(np.asarray(x, np.float32).astype(ml_dtypes.bfloat16).astype(np.float64), axis, -1)
    blocks = v.reshape(v.shape[:-1] + (-1, 32))
    amax = np.abs(blocks).max(-1, keepdims=True)
    byte = np.maximum(np.where(amax > 0, np.frexp(amax)[1] - 1 + 127, 0) - down, 1)
    scale = np.exp2(byte - 127.0)
    codes = (blocks / scale).astype(np.float32).astype(dtype).astype(np.float64)
    return np.moveaxis((codes * scale).reshape(v.shape), -1, axis)


WIDE = False


def mx_kscale(k):
    if not WIDE:
        return np.ones(k)
    levels = np.array([10, -10, 5, -5, 0])
    if k % 512:
        return np.exp2(np.random.permutation(np.resize(levels, k // 32))).repeat(32)
    a = np.empty((k // 512, 16))
    for p in range(k // 512):
        a[p, :8] = np.random.permutation(np.resize(levels, 8))
        for g in range(8):
            far = levels[np.abs(levels - a[p, g]) >= 10]
            a[p, g + 8] = far[np.random.randint(len(far))]
    return np.exp2(a.ravel()).repeat(32)


BF16 = ml_dtypes.bfloat16


def bf(x):
    return np.asarray(x, np.float32).astype(BF16)


def f64(x):
    return np.asarray(x).astype(np.float64)


B, NB, NL, NG, NK = 4096, 512, 1536, 500, 3
N2 = 2 * NB


def setup_inputs():
    s = mx_kscale(N2)
    r = s[:NB]
    return {'Volt': bf(np.random.standard_normal((B, N2)) * s),
            'Y_top': bf(np.random.standard_normal((NB, N2)) * 4.0 / np.sqrt(N2) / s[None, :] / r[:, None]),
            'Yconj_top': bf(np.random.standard_normal((NB, N2)) * 4.0 / np.sqrt(N2) / s[None, :] / r[:, None]),
            'PQ_Loads': bf(np.random.standard_normal((B, N2))),
            'PQ_Gens': bf(np.random.standard_normal((B, N2)))}


def reference(Volt, Y_top, Yconj_top, PQ_Loads, PQ_Gens):
    V = f64(Volt)
    Vq = mxq(V, 1, 'e4m3')
    YV = Vq @ mxq(f64(Y_top), 1, 'e4m3').T
    YcV = Vq @ mxq(f64(Yconj_top), 1, 'e4m3').T
    out = np.sum(V[:, :NB] * YV, axis=1) + np.sum(V[:, :NB] * YcV, axis=1)
    pq = f64(PQ_Loads) - f64(PQ_Gens)
    return out + np.sum(pq[:, :NB], axis=1) + np.sum(pq[:, NB:], axis=1)

@@ -1,0 +1,298 @@
+from contextlib import ExitStack
+
+import concourse.mybir as mybir
+from concourse.masks import make_identity
+
+F32 = mybir.dt.float32
+BF16 = mybir.dt.bfloat16
+U32 = mybir.dt.uint32
+U8 = mybir.dt.uint8
+FP8X4 = mybir.dt.float8_e4m3fn_x4
+ALU = mybir.AluOpType
+ACT = mybir.ActivationFunctionType
+AX = mybir.AxisListType
+
+P = 128
+B = 4096
+K = 1024
+NB = 512
+TILES = B // P
+CH = 4
+NCH = TILES // CH
+FLOPS = 2 * B * K * (2 * NB)
+
+PIN = False
+PQ_BUFS = 5
+G_TILES = []
+TO_VECTOR = [(29, 1), (31, 1)]
+TO_SCALAR = []
+V_D = [4, 4, 4, 4, 4, 5, 5, 5]
+A_AT = {3: 11, 6: 23}
+A_TILES = [11, 23]
+S_D = [3, 3, 4, 3, 4, 4, 4, 4]
+G_D = [0, 0, 0, 0, 0, 0, 0, 0]
+LOADS_TOP = ["V0a", "V0b", "V1", "L0", "G0", "V2", "L1", "G1", "V3", "L2", "G2", "V4", "L3", "G3", "V5", "L4"]
+LOADS_AFTER_Y = ["V6", "G4"]
+LOADS_AT = {1: ["L5"], 2: ["L6", "G5", "V7"], 4: ["L7", "G6", "G7a", "G7c", "G7d"]}
+SPREAD_ORDER = [1, 2, 3, 4, 0]
+
+
+def tile_kktloss_pc_t_kernel(tc, Volt, Y_top, Yconj_top, PQ_Loads, PQ_Gens, out):
+    nc = tc.nc
+    with ExitStack() as ctx:
+        if PIN:
+            ctx.enter_context(tc.manual_schedule())
+        const = ctx.enter_context(tc.tile_pool(name="const", bufs=1))
+        big = ctx.enter_context(tc.tile_pool(name="big", bufs=8))
+        pqp = ctx.enter_context(tc.tile_pool(name="pqp", bufs=PQ_BUFS))
+        work = ctx.enter_context(tc.tile_pool(name="work", bufs=3))
+        junk = ctx.enter_context(tc.tile_pool(name="junk", bufs=2))
+        psum = ctx.enter_context(tc.psum_pool(name="psum", bufs=4))
+
+        views = {
+            "V": Volt.rearrange("(p t) k -> p t k", t=TILES),
+            "L": PQ_Loads.rearrange("(p t) k -> p t k", t=TILES),
+            "G": PQ_Gens.rearrange("(p t) k -> p t k", t=TILES),
+        }
+        parts = {"": (0, 4), "a": (0, 2), "b": (2, 4), "c": (2, 3), "d": (3, 4)}
+        held = {}
+
+        def load(token):
+            kind, n, piece = token[0], int(token[1]), token[2:]
+            if (kind, n) not in held:
+                if kind == "V":
+                    held[(kind, n)] = big.tile([P, CH, K], BF16, tag="v", name="v%d" % n)
+                else:
+                    held[(kind, n)] = pqp.tile([P, CH, K], BF16, tag="pq" + kind, name="pq%s%d" % (kind, n))
+            lo, hi = parts[piece]
+            nc.sync.dma_start(out=held[(kind, n)][:, lo:hi, :], in_=views[kind][:, n * CH + lo:n * CH + hi, :])
+
+        def loads(tokens):
+            for token in tokens:
+                load(token)
+
+        y_raw = []
+        for mat, src in enumerate((Y_top, Yconj_top)):
+            raw = big.tile([P, CH, K], BF16, tag="v", name="yraw%d" % mat)
+            for r in range(CH):
+                nc.sync.dma_start(out=raw[:, r, :], in_=src[r * P:(r + 1) * P, :])
+            y_raw.append(raw)
+        loads(LOADS_TOP)
+
+        ident = const.tile([P, P], F32)
+        make_identity(nc, ident[:])
+        plus_one = const.tile([P, P], BF16)
+        make_identity(nc, plus_one[:])
+        minus_one = const.tile([P, P], BF16)
+        nc.gpsimd.tensor_scalar(out=minus_one[:], in0=plus_one[:], scalar1=-1.0, scalar2=0.0, op0=ALU.mult, op1=ALU.add)
+        y_codes = const.tile([P, 4 * NB], U32, align_bytes=64)
+        y_scales = const.tile([P, 4 * NB], U8, align_bytes=64)
+        acc_e = const.tile([P, TILES], F32)
+        acc_v = const.tile([P, 2, TILES], F32)
+        acc_s = const.tile([P, TILES], F32)
+        g_acc = const.tile([P, len(G_TILES), P], F32) if G_TILES else None
+        g_sum = const.tile([P, len(G_TILES)], F32) if G_TILES else None
+        nc.vector.memset(acc_v[:], 0.0)
+        nc.gpsimd.memset(acc_s[:], 0.0)
+
+        def transposes(raw, j):
+            tp = psum.tile([P, 4, P], F32, tag="tp", name="tp")
+            words = raw[:, j, :].bitcast(F32)
+            for q in range(4):
+                first = (q // 2) * 2 * P + q % 2
+                nc.tensor.transpose(tp[:, q, :], words[:, first:(q // 2 + 1) * 2 * P:2], ident[:])
+            return tp
+
+        for mat in range(2):
+            grp = work.tile([P, 4 * K], BF16, tag="grp", name="grpy", align_bytes=64)
+            g32 = grp[:].bitcast(F32).rearrange("p (g i u) -> p g i u", g=2, u=2)
+            for r in range(CH):
+                tp = transposes(y_raw[mat], r)
+                src = tp[:].rearrange("p (g u) b -> p g b u", u=2)
+                dst = g32[:, :, r * P:(r + 1) * P, :]
+                if r % 2 == 0:
+                    nc.scalar.copy(out=dst, in_=src)
+                else:
+                    nc.vector.tensor_copy(out=dst, in_=src)
+            for g in range(2):
+                c0 = (mat * 2 + g) * NB
+                nc.vector.quantize_mx(
+                    out=y_codes[:, c0:c0 + NB].bitcast(FP8X4),
+                    scales=y_scales[:, c0:c0 + NB],
+                    in_=grp[:, g * 4 * NB:(g + 1) * 4 * NB],
+                )
+        loads(LOADS_AFTER_Y)
+
+        front = {}
+
+        def t_chunk(n):
+            grp = work.tile([P, 4 * K], BF16, tag="grp", name="grpv", align_bytes=64)
+            codes = work.tile([P, K], U32, tag="codes", name="codes", align_bytes=64)
+            scales = work.tile([P, K], U8, tag="scales", name="scales", align_bytes=64)
+            tps = [transposes(held[("V", n)], j) for j in range(CH)]
+            front[n] = (grp, codes, scales, tps)
+
+        def e_chunk(n):
+            grp, codes, scales, tps = front[n]
+            for j in range(CH):
+                dst = grp[:, j * K:(j + 1) * K].bitcast(F32).rearrange("p (g b u) -> p g b u", g=2, u=2)
+                nc.scalar.copy(out=dst, in_=tps[j][:].rearrange("p (g u) b -> p g b u", u=2))
+
+        def q_part(n, j0, j1):
+            grp, codes, scales, tps = front[n]
+            nc.vector.quantize_mx(
+                out=codes[:, j0 * 256:j1 * 256].bitcast(FP8X4),
+                scales=scales[:, j0 * 256:j1 * 256],
+                in_=grp[:, j0 * K:j1 * K],
+            )
+
+        accs = {}
+
+        def m_chunk(n):
+            grp, codes, scales, tps = front[n]
+            for j in range(CH):
+                acc = psum.tile([P, NB], F32, tag="acc", name="acc")
+                i = 0
+                for g in range(2):
+                    c0 = j * 256 + g * P
+                    for mat in range(2):
+                        y0 = (mat * 2 + g) * NB
+                        nc.tensor.matmul_mx(
+                            out=acc[:],
+                            lhsT=codes[:, c0:c0 + P].bitcast(FP8X4),
+                            lhsT_scale=scales[:, c0:c0 + P],
+                            rhs=y_codes[:, y0:y0 + NB].bitcast(FP8X4),
+                            rhs_scale=y_scales[:, y0:y0 + NB],
+                            start=(i == 0),
+                            stop=(i == 3),
+                        )
+                        i += 1
+                accs[n * CH + j] = acc
+
+        def c_tile(t):
+            je = junk.tile([P, NB], F32, tag="je", name="je")
+            nc.vector.scalar_tensor_tensor(
+                out=je[:], in0=accs[t][:], scalar=1.0, in1=held[("V", t // CH)][:, t % CH, 0:NB],
+                op0=ALU.mult, op1=ALU.mult, accum_out=acc_e[:, t:t + 1],
+            )
+
+        v_units = []
+        s_units = []
+        for n in range(NCH):
+            for w in range(2):
+                for j in range(CH):
+                    t = n * CH + j
+                    if t in G_TILES or t in A_TILES:
+                        continue
+                    on_vector = (w == 0 and (t, w) not in TO_SCALAR) or (t, w) in TO_VECTOR
+                    if on_vector:
+                        v_units.append((t, w))
+                    else:
+                        s_units.append((t, w))
+        done = {"v": 0, "s": 0, "g": 0, "r": 0}
+
+        def unit_src(t, w):
+            return held[("LG"[w], t // CH)][:, t % CH, :]
+
+        def d_vector(count):
+            for unused in range(count):
+                if done["v"] < len(v_units):
+                    t, w = v_units[done["v"]]
+                    done["v"] += 1
+                    jv = junk.tile([P, K], BF16, tag="jv", name="jv")
+                    nc.vector.tensor_scalar(out=jv[:], in0=unit_src(t, w), scalar1=(1.0 - 2.0 * w), scalar2=None,
+                                            op0=ALU.mult, op1=ALU.add, accum_out=acc_v[:, w, t:t + 1])
+
+        def d_scalar(count):
+            for unused in range(count):
+                if done["s"] < len(s_units):
+                    t, w = s_units[done["s"]]
+                    done["s"] += 1
+                    js = junk.tile([P, K], BF16, tag="js", name="js")
+                    nc.scalar.activation(out=js[:], in_=unit_src(t, w), func=ACT.Copy, scale=(1.0 - 2.0 * w),
+                                         accum_out=acc_s[:, t:t + 1])
+
+        def d_gpsimd(count):
+            for unused in range(count):
+                if done["g"] < len(G_TILES):
+                    slot = done["g"]
+                    t = G_TILES[slot]
+                    done["g"] += 1
+                    pl, pg = unit_src(t, 0), unit_src(t, 1)
+                    gd = junk.tile([P, K], F32, tag="gd", name="gd")
+                    nc.gpsimd.tensor_tensor(out=gd[:, 0:512], in0=pl[:, 0:512], in1=pg[:, 0:512], op=ALU.subtract)
+                    nc.gpsimd.tensor_tensor(out=gd[:, 512:K], in0=pl[:, 512:K], in1=pg[:, 512:K], op=ALU.subtract)
+                    ge = junk.tile([P, 512], F32, tag="ge", name="ge")
+                    nc.gpsimd.tensor_tensor(out=ge[:], in0=gd[:, 0:512], in1=gd[:, 512:K], op=ALU.add)
+                    gf = junk.tile([P, 256], F32, tag="gf", name="gf")
+                    nc.gpsimd.tensor_tensor(out=gf[:], in0=ge[:, 0:256], in1=ge[:, 256:512], op=ALU.add)
+                    nc.gpsimd.tensor_tensor(out=g_acc[:, slot, :], in0=gf[:, 0:P], in1=gf[:, P:256], op=ALU.add)
+
+        def a_tile(t):
+            acc = psum.tile([P, NB], F32, tag="acc", name="acc")
+            for i in range(4):
+                w, c = i // 2, i % 2
+                nc.tensor.matmul(out=acc[:], lhsT=(plus_one if w == 0 else minus_one)[:],
+                                 rhs=unit_src(t, w)[:, c * NB:(c + 1) * NB], start=(i == 0), stop=(i == 3))
+            accs[("a", t)] = acc
+
+        def r_tile(t):
+            jr = junk.tile([P, NB], F32, tag="jr", name="jr")
+            nc.scalar.activation(out=jr[:], in_=accs[("a", t)][:], func=ACT.Copy, accum_out=acc_s[:, t:t + 1])
+
+        def g_reduce():
+            slot = done["r"]
+            done["r"] += 1
+            nc.vector.tensor_reduce(out=g_sum[:, slot:slot + 1], in_=g_acc[:, slot, :], axis=AX.X, op=ALU.add)
+
+        t_chunk(0)
+        e_chunk(0)
+        for j in range(CH):
+            q_part(0, j, j + 1)
+        for n in range(NCH):
+            loads(LOADS_AT.get(n, []))
+            more = n + 1 < NCH
+            if more:
+                t_chunk(n + 1)
+            m_chunk(n)
+            if n in A_AT:
+                a_tile(A_AT[n])
+            if more:
+                e_chunk(n + 1)
+            d_scalar(S_D[n])
+            if n in A_AT:
+                r_tile(A_AT[n])
+            d_gpsimd(G_D[n])
+            slots = [0, 0, 0, 0, 0]
+            for i in range(V_D[n]):
+                slots[SPREAD_ORDER[i % 5]] += 1
+            d_vector(slots[0])
+            if more:
+                q_part(n + 1, 0, 2)
+            d_vector(slots[1])
+            if more:
+                q_part(n + 1, 2, 4)
+            c_tile(n * CH)
+            c_tile(n * CH + 1)
+            d_vector(slots[2])
+            c_tile(n * CH + 2)
+            d_vector(slots[3])
+            c_tile(n * CH + 3)
+            d_vector(slots[4])
+            if done["g"] - done["r"] > 1:
+                g_reduce()
+        d_scalar(len(s_units))
+        d_vector(len(v_units) - done["v"] - len(TO_VECTOR))
+        part = const.tile([P, TILES], F32)
+        nc.vector.tensor_tensor(out=part[:], in0=acc_v[:, 0, :], in1=acc_e[:], op=ALU.add)
+        d_vector(len(TO_VECTOR))
+        for unused in range(len(G_TILES) - done["r"]):
+            g_reduce()
+
+        nc.vector.tensor_tensor(out=part[:], in0=part[:], in1=acc_v[:, 1, :], op=ALU.add)
+        if G_TILES:
+            lanes = part[:].rearrange("p (n j) -> p n j", j=CH)[:, 0:len(G_TILES), 3]
+            nc.vector.tensor_tensor(out=lanes, in0=lanes, in1=g_sum[:], op=ALU.add)
+        res = const.tile([P, TILES], F32)
+        nc.vector.tensor_tensor(out=res[:], in0=part[:], in1=acc_s[:], op=ALU.add)
+        nc.sync.dma_start(out=out.rearrange("(p t) -> p t", t=TILES), in_=res[:])

@@ -21,31 +21,25 @@ CH = 4
 NCH = TILES // CH
 FLOPS = 2 * B * K * (2 * NB)
 
-PIN = False
-PQ_BUFS = 5
+PERM_V = ()
 G_TILES = []
-TO_VECTOR = [(29, 1), (31, 1)]
-TO_SCALAR = []
-V_D = [4, 4, 4, 4, 4, 5, 5, 5]
-A_AT = {3: 11, 6: 23}
-A_TILES = [11, 23]
-S_D = [3, 3, 4, 3, 4, 4, 4, 4]
-G_D = [0, 0, 0, 0, 0, 0, 0, 0]
-LOADS_TOP = ["V0a", "V0b", "V1", "L0", "G0", "V2", "L1", "G1", "V3", "L2", "G2", "V4", "L3", "G3", "V5", "L4"]
-LOADS_AFTER_Y = ["V6", "G4"]
-LOADS_AT = {1: ["L5"], 2: ["L6", "G5", "V7"], 4: ["L7", "G6", "G7a", "G7c", "G7d"]}
-SPREAD_ORDER = [1, 2, 3, 4, 0]
+G_AT = {1: 1, 2: 1, 3: 1, 4: 1, 5: 1, 6: 1}
+G_SPLIT = 512
+V_UNITS = [2,4,4,4,4,4,4,3]
+V_SPREAD = [0, 2, 3, 1, 4, 0]
+S_UNITS = [3,4,3,4,4,4,4,5]
+LOADS = ["V1a", "V1b", "L0", "V2", "G0", "L1", "V3", "G1", "L2", "V4", "G2", "L3", "V5", "G3", "L4", "V6", "G4", "L5", "V7", "G5", "L6", "G6", "L7", "G7a", "G7b"]
 
 
 def tile_kktloss_pc_t_kernel(tc, Volt, Y_top, Yconj_top, PQ_Loads, PQ_Gens, out):
     nc = tc.nc
     with ExitStack() as ctx:
-        if PIN:
-            ctx.enter_context(tc.manual_schedule())
+        ctx.enter_context(tc.manual_schedule())
         const = ctx.enter_context(tc.tile_pool(name="const", bufs=1))
-        big = ctx.enter_context(tc.tile_pool(name="big", bufs=8))
-        pqp = ctx.enter_context(tc.tile_pool(name="pqp", bufs=PQ_BUFS))
+        big = ctx.enter_context(tc.tile_pool(name="big", bufs=9))
+        pqp = ctx.enter_context(tc.tile_pool(name="pqp", bufs=5))
         work = ctx.enter_context(tc.tile_pool(name="work", bufs=3))
+        perm = ctx.enter_context(tc.tile_pool(name="perm", bufs=4))
         junk = ctx.enter_context(tc.tile_pool(name="junk", bufs=2))
         psum = ctx.enter_context(tc.psum_pool(name="psum", bufs=4))
 
@@ -54,22 +48,15 @@ def tile_kktloss_pc_t_kernel(tc, Volt, Y_top, Yconj_top, PQ_Loads, PQ_Gens, out)
             "L": PQ_Loads.rearrange("(p t) k -> p t k", t=TILES),
             "G": PQ_Gens.rearrange("(p t) k -> p t k", t=TILES),
         }
-        parts = {"": (0, 4), "a": (0, 2), "b": (2, 4), "c": (2, 3), "d": (3, 4)}
         held = {}
 
-        def load(token):
-            kind, n, piece = token[0], int(token[1]), token[2:]
+        def load(kind, n, lo, hi):
             if (kind, n) not in held:
                 if kind == "V":
                     held[(kind, n)] = big.tile([P, CH, K], BF16, tag="v", name="v%d" % n)
                 else:
                     held[(kind, n)] = pqp.tile([P, CH, K], BF16, tag="pq" + kind, name="pq%s%d" % (kind, n))
-            lo, hi = parts[piece]
             nc.sync.dma_start(out=held[(kind, n)][:, lo:hi, :], in_=views[kind][:, n * CH + lo:n * CH + hi, :])
-
-        def loads(tokens):
-            for token in tokens:
-                load(token)
 
         y_raw = []
         for mat, src in enumerate((Y_top, Yconj_top)):
@@ -77,51 +64,59 @@ def tile_kktloss_pc_t_kernel(tc, Volt, Y_top, Yconj_top, PQ_Loads, PQ_Gens, out)
             for r in range(CH):
                 nc.sync.dma_start(out=raw[:, r, :], in_=src[r * P:(r + 1) * P, :])
             y_raw.append(raw)
-        loads(LOADS_TOP)
+        for j in range(CH):
+            load("V", 0, j, j + 1)
+        for token in LOADS:
+            lo, hi = {"": (0, 4), "a": (0, 2), "b": (2, 4)}[token[2:]]
+            load(token[0], int(token[1]), lo, hi)
 
         ident = const.tile([P, P], F32)
         make_identity(nc, ident[:])
-        plus_one = const.tile([P, P], BF16)
-        make_identity(nc, plus_one[:])
-        minus_one = const.tile([P, P], BF16)
-        nc.gpsimd.tensor_scalar(out=minus_one[:], in0=plus_one[:], scalar1=-1.0, scalar2=0.0, op0=ALU.mult, op1=ALU.add)
         y_codes = const.tile([P, 4 * NB], U32, align_bytes=64)
         y_scales = const.tile([P, 4 * NB], U8, align_bytes=64)
-        acc_e = const.tile([P, TILES], F32)
-        acc_v = const.tile([P, 2, TILES], F32)
-        acc_s = const.tile([P, TILES], F32)
-        g_acc = const.tile([P, len(G_TILES), P], F32) if G_TILES else None
-        g_sum = const.tile([P, len(G_TILES)], F32) if G_TILES else None
-        nc.vector.memset(acc_v[:], 0.0)
-        nc.gpsimd.memset(acc_s[:], 0.0)
+        sums = const.tile([P, TILES, 3], F32)
+        if G_TILES:
+            nc.vector.memset(sums[:, :, 1:2], 0.0)
 
-        def transposes(raw, j):
-            tp = psum.tile([P, 4, P], F32, tag="tp", name="tp")
+        def permute(raw, j):
+            pw = perm.tile([P, 2, 2, P], F32, tag="pw", name="pw")
+            nc.vector.tensor_copy(out=pw[:], in_=raw[:, j, :].bitcast(F32).rearrange("p (g w u) -> p g u w", g=2, u=2))
+            return pw
+
+        def transposes(raw, j, pw, tag):
+            tp = psum.tile([P, 4, P], F32, tag=tag, name="tp" + tag)
             words = raw[:, j, :].bitcast(F32)
             for q in range(4):
-                first = (q // 2) * 2 * P + q % 2
-                nc.tensor.transpose(tp[:, q, :], words[:, first:(q // 2 + 1) * 2 * P:2], ident[:])
+                g, u = q // 2, q % 2
+                if pw is not None:
+                    src = pw[:, g, u, :]
+                else:
+                    src = words[:, g * 256 + u:(g + 1) * 256:2]
+                nc.tensor.transpose(tp[:, q, :], src, ident[:])
             return tp
 
+        y_grp = []
         for mat in range(2):
             grp = work.tile([P, 4 * K], BF16, tag="grp", name="grpy", align_bytes=64)
+            y_grp.append(grp)
             g32 = grp[:].bitcast(F32).rearrange("p (g i u) -> p g i u", g=2, u=2)
             for r in range(CH):
-                tp = transposes(y_raw[mat], r)
+                tp = transposes(y_raw[mat], r, None, ("tp", "acc")[mat])
                 src = tp[:].rearrange("p (g u) b -> p g b u", u=2)
                 dst = g32[:, :, r * P:(r + 1) * P, :]
-                if r % 2 == 0:
-                    nc.scalar.copy(out=dst, in_=src)
-                else:
+                if r == 3:
                     nc.vector.tensor_copy(out=dst, in_=src)
+                else:
+                    nc.scalar.copy(out=dst, in_=src)
+
+        def quantize_y(mat):
             for g in range(2):
                 c0 = (mat * 2 + g) * NB
                 nc.vector.quantize_mx(
                     out=y_codes[:, c0:c0 + NB].bitcast(FP8X4),
                     scales=y_scales[:, c0:c0 + NB],
-                    in_=grp[:, g * 4 * NB:(g + 1) * 4 * NB],
+                    in_=y_grp[mat][:, g * 4 * NB:(g + 1) * 4 * NB],
                 )
-        loads(LOADS_AFTER_Y)
 
         front = {}
 
@@ -129,33 +124,27 @@ def tile_kktloss_pc_t_kernel(tc, Volt, Y_top, Yconj_top, PQ_Loads, PQ_Gens, out)
             grp = work.tile([P, 4 * K], BF16, tag="grp", name="grpv", align_bytes=64)
             codes = work.tile([P, K], U32, tag="codes", name="codes", align_bytes=64)
             scales = work.tile([P, K], U8, tag="scales", name="scales", align_bytes=64)
-            tps = [transposes(held[("V", n)], j) for j in range(CH)]
-            front[n] = (grp, codes, scales, tps)
-
-        def e_chunk(n):
-            grp, codes, scales, tps = front[n]
+            front[n] = (grp, codes, scales)
             for j in range(CH):
+                pw = permute(held[("V", n)], j) if n in PERM_V else None
+                tp = transposes(held[("V", n)], j, pw, "tp")
                 dst = grp[:, j * K:(j + 1) * K].bitcast(F32).rearrange("p (g b u) -> p g b u", g=2, u=2)
-                nc.scalar.copy(out=dst, in_=tps[j][:].rearrange("p (g u) b -> p g b u", u=2))
+                nc.scalar.copy(out=dst, in_=tp[:].rearrange("p (g u) b -> p g b u", u=2))
 
-        def q_part(n, j0, j1):
-            grp, codes, scales, tps = front[n]
-            nc.vector.quantize_mx(
-                out=codes[:, j0 * 256:j1 * 256].bitcast(FP8X4),
-                scales=scales[:, j0 * 256:j1 * 256],
-                in_=grp[:, j0 * K:j1 * K],
-            )
+        def q_chunk(n):
+            grp, codes, scales = front[n]
+            nc.vector.quantize_mx(out=codes[:].bitcast(FP8X4), scales=scales[:], in_=grp[:])
 
         accs = {}
 
         def m_chunk(n):
-            grp, codes, scales, tps = front[n]
+            grp, codes, scales = front[n]
             for j in range(CH):
                 acc = psum.tile([P, NB], F32, tag="acc", name="acc")
                 i = 0
-                for g in range(2):
-                    c0 = j * 256 + g * P
-                    for mat in range(2):
+                for mat in range(2):
+                    for g in range(2):
+                        c0 = j * 256 + g * P
                         y0 = (mat * 2 + g) * NB
                         nc.tensor.matmul_mx(
                             out=acc[:],
@@ -173,126 +162,89 @@ def tile_kktloss_pc_t_kernel(tc, Volt, Y_top, Yconj_top, PQ_Loads, PQ_Gens, out)
             je = junk.tile([P, NB], F32, tag="je", name="je")
             nc.vector.scalar_tensor_tensor(
                 out=je[:], in0=accs[t][:], scalar=1.0, in1=held[("V", t // CH)][:, t % CH, 0:NB],
-                op0=ALU.mult, op1=ALU.mult, accum_out=acc_e[:, t:t + 1],
+                op0=ALU.mult, op1=ALU.mult, accum_out=sums[:, t, 2:3],
             )
 
-        v_units = []
-        s_units = []
-        for n in range(NCH):
-            for w in range(2):
-                for j in range(CH):
-                    t = n * CH + j
-                    if t in G_TILES or t in A_TILES:
-                        continue
-                    on_vector = (w == 0 and (t, w) not in TO_SCALAR) or (t, w) in TO_VECTOR
-                    if on_vector:
-                        v_units.append((t, w))
-                    else:
-                        s_units.append((t, w))
-        done = {"v": 0, "s": 0, "g": 0, "r": 0}
+        units = []
+        for token in LOADS:
+            if token[0] != "V":
+                n = int(token[1])
+                lo, hi = {"": (0, 4), "a": (0, 2), "b": (2, 4)}[token[2:]]
+                units.extend([(n * CH + j, "LG".index(token[0])) for j in range(lo, hi) if n * CH + j not in G_TILES])
+        units.reverse()
 
-        def unit_src(t, w):
-            return held[("LG"[w], t // CH)][:, t % CH, :]
+        def d_vector():
+            if units:
+                t, w = units.pop()
+                jv = junk.tile([P, K], BF16, tag="jv", name="jv")
+                nc.vector.tensor_scalar(out=jv[:], in0=held[("LG"[w], t // CH)][:, t % CH, :], scalar1=(1.0 - 2.0 * w),
+                                        scalar2=None, op0=ALU.mult, op1=ALU.add, accum_out=sums[:, t, w:w + 1])
 
-        def d_vector(count):
-            for unused in range(count):
-                if done["v"] < len(v_units):
-                    t, w = v_units[done["v"]]
-                    done["v"] += 1
-                    jv = junk.tile([P, K], BF16, tag="jv", name="jv")
-                    nc.vector.tensor_scalar(out=jv[:], in0=unit_src(t, w), scalar1=(1.0 - 2.0 * w), scalar2=None,
-                                            op0=ALU.mult, op1=ALU.add, accum_out=acc_v[:, w, t:t + 1])
+        def d_scalar():
+            if units:
+                t, w = units.pop()
+                js = junk.tile([P, K], BF16, tag="js", name="js")
+                nc.scalar.activation(out=js[:], in_=held[("LG"[w], t // CH)][:, t % CH, :], func=ACT.Copy,
+                                     scale=(1.0 - 2.0 * w), accum_out=sums[:, t, w:w + 1])
 
-        def d_scalar(count):
-            for unused in range(count):
-                if done["s"] < len(s_units):
-                    t, w = s_units[done["s"]]
-                    done["s"] += 1
-                    js = junk.tile([P, K], BF16, tag="js", name="js")
-                    nc.scalar.activation(out=js[:], in_=unit_src(t, w), func=ACT.Copy, scale=(1.0 - 2.0 * w),
-                                         accum_out=acc_s[:, t:t + 1])
+        g_acc = const.tile([P, max(len(G_TILES), 1), P], F32)
+        g_left = list(G_TILES)
 
-        def d_gpsimd(count):
-            for unused in range(count):
-                if done["g"] < len(G_TILES):
-                    slot = done["g"]
-                    t = G_TILES[slot]
-                    done["g"] += 1
-                    pl, pg = unit_src(t, 0), unit_src(t, 1)
-                    gd = junk.tile([P, K], F32, tag="gd", name="gd")
-                    nc.gpsimd.tensor_tensor(out=gd[:, 0:512], in0=pl[:, 0:512], in1=pg[:, 0:512], op=ALU.subtract)
-                    nc.gpsimd.tensor_tensor(out=gd[:, 512:K], in0=pl[:, 512:K], in1=pg[:, 512:K], op=ALU.subtract)
-                    ge = junk.tile([P, 512], F32, tag="ge", name="ge")
-                    nc.gpsimd.tensor_tensor(out=ge[:], in0=gd[:, 0:512], in1=gd[:, 512:K], op=ALU.add)
-                    gf = junk.tile([P, 256], F32, tag="gf", name="gf")
-                    nc.gpsimd.tensor_tensor(out=gf[:], in0=ge[:, 0:256], in1=ge[:, 256:512], op=ALU.add)
-                    nc.gpsimd.tensor_tensor(out=g_acc[:, slot, :], in0=gf[:, 0:P], in1=gf[:, P:256], op=ALU.add)
+        def g_tile():
+            if not g_left:
+                return
+            t = g_left.pop(0)
+            slot = G_TILES.index(t)
+            pl, pg = held[("L", t // CH)][:, t % CH, :], held[("G", t // CH)][:, t % CH, :]
+            gd = junk.tile([P, K], F32, tag="gd", name="gd")
+            for c in range(0, K, G_SPLIT):
+                nc.gpsimd.tensor_tensor(out=gd[:, c:c + G_SPLIT], in0=pl[:, c:c + G_SPLIT], in1=pg[:, c:c + G_SPLIT], op=ALU.subtract)
+            width = K // 2
+            while width > P:
+                for c in range(0, width, G_SPLIT):
+                    step = min(G_SPLIT, width)
+                    nc.gpsimd.tensor_tensor(out=gd[:, c:c + step], in0=gd[:, c:c + step], in1=gd[:, width + c:width + c + step], op=ALU.add)
+                width //= 2
+            nc.gpsimd.tensor_tensor(out=g_acc[:, slot, :], in0=gd[:, 0:P], in1=gd[:, P:2 * P], op=ALU.add)
 
-        def a_tile(t):
-            acc = psum.tile([P, NB], F32, tag="acc", name="acc")
-            for i in range(4):
-                w, c = i // 2, i % 2
-                nc.tensor.matmul(out=acc[:], lhsT=(plus_one if w == 0 else minus_one)[:],
-                                 rhs=unit_src(t, w)[:, c * NB:(c + 1) * NB], start=(i == 0), stop=(i == 3))
-            accs[("a", t)] = acc
-
-        def r_tile(t):
-            jr = junk.tile([P, NB], F32, tag="jr", name="jr")
-            nc.scalar.activation(out=jr[:], in_=accs[("a", t)][:], func=ACT.Copy, accum_out=acc_s[:, t:t + 1])
-
-        def g_reduce():
-            slot = done["r"]
-            done["r"] += 1
-            nc.vector.tensor_reduce(out=g_sum[:, slot:slot + 1], in_=g_acc[:, slot, :], axis=AX.X, op=ALU.add)
-
+        quantize_y(0)
         t_chunk(0)
-        e_chunk(0)
-        for j in range(CH):
-            q_part(0, j, j + 1)
+        quantize_y(1)
+        q_chunk(0)
         for n in range(NCH):
-            loads(LOADS_AT.get(n, []))
             more = n + 1 < NCH
             if more:
                 t_chunk(n + 1)
             m_chunk(n)
-            if n in A_AT:
-                a_tile(A_AT[n])
-            if more:
-                e_chunk(n + 1)
-            d_scalar(S_D[n])
-            if n in A_AT:
-                r_tile(A_AT[n])
-            d_gpsimd(G_D[n])
+            s_left = S_UNITS[n]
+            for unused in range(G_AT.get(n, 0)):
+                g_tile()
             slots = [0, 0, 0, 0, 0]
-            for i in range(V_D[n]):
-                slots[SPREAD_ORDER[i % 5]] += 1
-            d_vector(slots[0])
-            if more:
-                q_part(n + 1, 0, 2)
-            d_vector(slots[1])
-            if more:
-                q_part(n + 1, 2, 4)
-            c_tile(n * CH)
-            c_tile(n * CH + 1)
-            d_vector(slots[2])
-            c_tile(n * CH + 2)
-            d_vector(slots[3])
-            c_tile(n * CH + 3)
-            d_vector(slots[4])
-            if done["g"] - done["r"] > 1:
-                g_reduce()
-        d_scalar(len(s_units))
-        d_vector(len(v_units) - done["v"] - len(TO_VECTOR))
-        part = const.tile([P, TILES], F32)
-        nc.vector.tensor_tensor(out=part[:], in0=acc_v[:, 0, :], in1=acc_e[:], op=ALU.add)
-        d_vector(len(TO_VECTOR))
-        for unused in range(len(G_TILES) - done["r"]):
-            g_reduce()
-
-        nc.vector.tensor_tensor(out=part[:], in0=part[:], in1=acc_v[:, 1, :], op=ALU.add)
-        if G_TILES:
-            lanes = part[:].rearrange("p (n j) -> p n j", j=CH)[:, 0:len(G_TILES), 3]
-            nc.vector.tensor_tensor(out=lanes, in0=lanes, in1=g_sum[:], op=ALU.add)
+            for i in range(V_UNITS[n]):
+                slots[V_SPREAD[i % 6]] += 1
+            plan = ["d"] * slots[0] + ["q"] + ["d"] * slots[1] + [0] + ["d"] * slots[2] + [1] + ["d"] * slots[3] + [2] + ["d"] * slots[4] + [3]
+            for step in plan:
+                if step == "d":
+                    d_vector()
+                    if s_left:
+                        s_left -= 1
+                        d_scalar()
+                elif step == "q":
+                    if more:
+                        q_chunk(n + 1)
+                else:
+                    c_tile(n * CH + step)
+            for unused in range(s_left):
+                d_scalar()
+        for slot, t in enumerate(G_TILES):
+            nc.vector.tensor_reduce(out=sums[:, t, 0:1], in_=g_acc[:, slot, :], axis=AX.X, op=ALU.add)
+        turn = 0
+        while units:
+            if turn % 2 == 0:
+                d_scalar()
+            else:
+                d_vector()
+            turn += 1
         res = const.tile([P, TILES], F32)
-        nc.vector.tensor_tensor(out=res[:], in0=part[:], in1=acc_s[:], op=ALU.add)
+        nc.vector.tensor_reduce(out=res[:], in_=sums[:], axis=AX.X, op=ALU.add)
         nc.sync.dma_start(out=out.rearrange("(p t) -> p t", t=TILES), in_=res[:])

@@ -22,13 +22,22 @@ NCH = TILES // CH
 FLOPS = 2 * B * K * (2 * NB)
 
 PERM_V = ()
-G_TILES = []
-G_AT = {1: 1, 2: 1, 3: 1, 4: 1, 5: 1, 6: 1}
+WARM_START = 0
+WARM_EVERY = 0
+WARM_CHUNKS = (0, 1)
+PERM_G = {}
+G_TILES = [15,19,22,26]
+G_AT = {4:1,5:1, 6: 2}
 G_SPLIT = 512
-V_UNITS = [2,4,4,4,4,4,4,3]
+PRE = []
+V_PRE = 0
+S_PRE = 0
+V_MID = 0
+Y_ON_V = (3,)
+V_UNITS = [2,4,4,4,3,3,3,3]
 V_SPREAD = [0, 2, 3, 1, 4, 0]
-S_UNITS = [3,4,3,4,4,4,4,5]
-LOADS = ["V1a", "V1b", "L0", "V2", "G0", "L1", "V3", "G1", "L2", "V4", "G2", "L3", "V5", "G3", "L4", "V6", "G4", "L5", "V7", "G5", "L6", "G6", "L7", "G7a", "G7b"]
+S_UNITS = [3,4,3,4,3,4,4,4]
+LOADS = ["V1a", "V1b", "L0", "V2", "G0", "L1", "G1a", "V3", "G1b", "L2", "G2a", "V4", "G2b", "L3", "G3a", "V5", "G3b", "L4", "G4a", "V6", "G4b", "L5", "G5a", "V7", "G5b", "L6", "G6", "L7", "G7a", "G7b"]
 
 
 def tile_kktloss_pc_t_kernel(tc, Volt, Y_top, Yconj_top, PQ_Loads, PQ_Gens, out):
@@ -58,6 +67,12 @@ def tile_kktloss_pc_t_kernel(tc, Volt, Y_top, Yconj_top, PQ_Loads, PQ_Gens, out)
                     held[(kind, n)] = pqp.tile([P, CH, K], BF16, tag="pq" + kind, name="pq%s%d" % (kind, n))
             nc.sync.dma_start(out=held[(kind, n)][:, lo:hi, :], in_=views[kind][:, n * CH + lo:n * CH + hi, :])
 
+        def load_token(token):
+            lo, hi = {"": (0, 4), "a": (0, 2), "b": (2, 4), "c": (0, 1), "d": (1, 2)}[token[2:]]
+            load(token[0], int(token[1]), lo, hi)
+
+        for token in PRE:
+            load_token(token)
         y_raw = []
         for mat, src in enumerate((Y_top, Yconj_top)):
             raw = big.tile([P, CH, K], BF16, tag="v", name="yraw%d" % mat)
@@ -67,8 +82,7 @@ def tile_kktloss_pc_t_kernel(tc, Volt, Y_top, Yconj_top, PQ_Loads, PQ_Gens, out)
         for j in range(CH):
             load("V", 0, j, j + 1)
         for token in LOADS:
-            lo, hi = {"": (0, 4), "a": (0, 2), "b": (2, 4)}[token[2:]]
-            load(token[0], int(token[1]), lo, hi)
+            load_token(token)
 
         ident = const.tile([P, P], F32)
         make_identity(nc, ident[:])
@@ -83,8 +97,21 @@ def tile_kktloss_pc_t_kernel(tc, Volt, Y_top, Yconj_top, PQ_Loads, PQ_Gens, out)
             nc.vector.tensor_copy(out=pw[:], in_=raw[:, j, :].bitcast(F32).rearrange("p (g w u) -> p g u w", g=2, u=2))
             return pw
 
-        def transposes(raw, j, pw, tag):
+        def permute_g(raw, j):
+            pw = perm.tile([P, 2, 2, P], F32, tag="pw", name="pwg")
+            words = raw[:, j, :].rearrange("p (g w u e) -> p g u w e", g=2, u=2, e=2)
+            for g in range(2):
+                nc.gpsimd.tensor_scalar(out=pw[:, g, :, :].rearrange("p u w -> p (u w)").bitcast(BF16).rearrange("p (u w e) -> p u w e", u=2, e=2),
+                                        in0=words[:, g], scalar1=1.0, scalar2=0.0, op0=ALU.mult, op1=ALU.add)
+            return pw
+
+        idle = const.tile([P, NB], BF16)
+        nc.vector.memset(idle[:], 0.0)
+
+        def transposes(raw, j, pw, tag, warm=0):
             tp = psum.tile([P, 4, P], F32, tag=tag, name="tp" + tag)
+            for unused in range(warm):
+                nc.tensor.matmul(out=tp[:].rearrange("p q b -> p (q b)"), lhsT=idle[:, 0:P], rhs=idle[:], start=True, stop=True)
             words = raw[:, j, :].bitcast(F32)
             for q in range(4):
                 g, u = q // 2, q % 2
@@ -95,16 +122,46 @@ def tile_kktloss_pc_t_kernel(tc, Volt, Y_top, Yconj_top, PQ_Loads, PQ_Gens, out)
                 nc.tensor.transpose(tp[:, q, :], src, ident[:])
             return tp
 
+        units = []
+        for token in PRE + LOADS:
+            if token[0] != "V":
+                n = int(token[1])
+                lo, hi = {"": (0, 4), "a": (0, 2), "b": (2, 4), "c": (0, 1), "d": (1, 2)}[token[2:]]
+                units.extend([(n * CH + j, "LG".index(token[0])) for j in range(lo, hi) if n * CH + j not in G_TILES])
+        units.reverse()
+
+        def d_vector():
+            if units:
+                t, w = units.pop()
+                jv = junk.tile([P, K], BF16, tag="jv", name="jv")
+                nc.vector.tensor_scalar(out=jv[:], in0=held[("LG"[w], t // CH)][:, t % CH, :], scalar1=(1.0 - 2.0 * w),
+                                        scalar2=None, op0=ALU.mult, op1=ALU.add, accum_out=sums[:, t, w:w + 1])
+
+        def d_scalar():
+            if units:
+                t, w = units.pop()
+                js = junk.tile([P, K], BF16, tag="js", name="js")
+                nc.scalar.activation(out=js[:], in_=held[("LG"[w], t // CH)][:, t % CH, :], func=ACT.Copy,
+                                     scale=(1.0 - 2.0 * w), accum_out=sums[:, t, w:w + 1])
+
+        for unused in range(V_PRE):
+            d_vector()
+        for unused in range(S_PRE):
+            d_scalar()
+
         y_grp = []
         for mat in range(2):
             grp = work.tile([P, 4 * K], BF16, tag="grp", name="grpy", align_bytes=64)
             y_grp.append(grp)
             g32 = grp[:].bitcast(F32).rearrange("p (g i u) -> p g i u", g=2, u=2)
             for r in range(CH):
-                tp = transposes(y_raw[mat], r, None, ("tp", "acc")[mat])
+                warm = 1 if WARM_EVERY and r % WARM_EVERY == 0 else 0
+                if mat == 0 and r == 0:
+                    warm = WARM_START
+                tp = transposes(y_raw[mat], r, None, ("tp", "acc")[mat], warm)
                 src = tp[:].rearrange("p (g u) b -> p g b u", u=2)
                 dst = g32[:, :, r * P:(r + 1) * P, :]
-                if r == 3:
+                if r in Y_ON_V:
                     nc.vector.tensor_copy(out=dst, in_=src)
                 else:
                     nc.scalar.copy(out=dst, in_=src)
@@ -120,14 +177,20 @@ def tile_kktloss_pc_t_kernel(tc, Volt, Y_top, Yconj_top, PQ_Loads, PQ_Gens, out)
 
         front = {}
 
+        pws = {}
+
+        def p_chunk(n):
+            for j in PERM_G.get(n, ()):
+                pws[(n, j)] = permute_g(held[("V", n)], j)
+
         def t_chunk(n):
             grp = work.tile([P, 4 * K], BF16, tag="grp", name="grpv", align_bytes=64)
             codes = work.tile([P, K], U32, tag="codes", name="codes", align_bytes=64)
             scales = work.tile([P, K], U8, tag="scales", name="scales", align_bytes=64)
             front[n] = (grp, codes, scales)
             for j in range(CH):
-                pw = permute(held[("V", n)], j) if n in PERM_V else None
-                tp = transposes(held[("V", n)], j, pw, "tp")
+                pw = pws.pop((n, j)) if (n, j) in pws else None
+                tp = transposes(held[("V", n)], j, pw, "tp", 1 if WARM_EVERY and n in WARM_CHUNKS and j % WARM_EVERY == 0 else 0)
                 dst = grp[:, j * K:(j + 1) * K].bitcast(F32).rearrange("p (g b u) -> p g b u", g=2, u=2)
                 nc.scalar.copy(out=dst, in_=tp[:].rearrange("p (g u) b -> p g b u", u=2))
 
@@ -165,28 +228,6 @@ def tile_kktloss_pc_t_kernel(tc, Volt, Y_top, Yconj_top, PQ_Loads, PQ_Gens, out)
                 op0=ALU.mult, op1=ALU.mult, accum_out=sums[:, t, 2:3],
             )
 
-        units = []
-        for token in LOADS:
-            if token[0] != "V":
-                n = int(token[1])
-                lo, hi = {"": (0, 4), "a": (0, 2), "b": (2, 4)}[token[2:]]
-                units.extend([(n * CH + j, "LG".index(token[0])) for j in range(lo, hi) if n * CH + j not in G_TILES])
-        units.reverse()
-
-        def d_vector():
-            if units:
-                t, w = units.pop()
-                jv = junk.tile([P, K], BF16, tag="jv", name="jv")
-                nc.vector.tensor_scalar(out=jv[:], in0=held[("LG"[w], t // CH)][:, t % CH, :], scalar1=(1.0 - 2.0 * w),
-                                        scalar2=None, op0=ALU.mult, op1=ALU.add, accum_out=sums[:, t, w:w + 1])
-
-        def d_scalar():
-            if units:
-                t, w = units.pop()
-                js = junk.tile([P, K], BF16, tag="js", name="js")
-                nc.scalar.activation(out=js[:], in_=held[("LG"[w], t // CH)][:, t % CH, :], func=ACT.Copy,
-                                     scale=(1.0 - 2.0 * w), accum_out=sums[:, t, w:w + 1])
-
         g_acc = const.tile([P, max(len(G_TILES), 1), P], F32)
         g_left = list(G_TILES)
 
@@ -208,6 +249,8 @@ def tile_kktloss_pc_t_kernel(tc, Volt, Y_top, Yconj_top, PQ_Loads, PQ_Gens, out)
             nc.gpsimd.tensor_tensor(out=g_acc[:, slot, :], in0=gd[:, 0:P], in1=gd[:, P:2 * P], op=ALU.add)
 
         quantize_y(0)
+        for unused in range(V_MID):
+            d_vector()
         t_chunk(0)
         quantize_y(1)
         q_chunk(0)
@@ -215,6 +258,8 @@ def tile_kktloss_pc_t_kernel(tc, Volt, Y_top, Yconj_top, PQ_Loads, PQ_Gens, out)
             more = n + 1 < NCH
             if more:
                 t_chunk(n + 1)
+            if n + 2 < NCH:
+                p_chunk(n + 2)
             m_chunk(n)
             s_left = S_UNITS[n]
             for unused in range(G_AT.get(n, 0)):

@@ -205,8 +205,8 @@ def tile_kktloss_pc_t_kernel(tc, Volt, Y_top, Yconj_top, PQ_Loads, PQ_Gens, out)
             for j in range(CH):
                 acc = psum.tile([P, NB], F32, tag="acc", name="acc")
                 i = 0
-                for mat in range(2):
-                    for g in range(2):
+                for g in range(2):
+                    for mat in range(2):
                         c0 = j * 256 + g * P
                         y0 = (mat * 2 + g) * NB
                         nc.tensor.matmul_mx(

from contextlib import ExitStack

import concourse.mybir as mybir
from concourse.masks import make_identity

F32 = mybir.dt.float32
BF16 = mybir.dt.bfloat16
U32 = mybir.dt.uint32
U8 = mybir.dt.uint8
FP8X4 = mybir.dt.float8_e4m3fn_x4
ALU = mybir.AluOpType
ACT = mybir.ActivationFunctionType
AX = mybir.AxisListType

P = 128
B = 4096
K = 1024
NB = 512
TILES = B // P
CH = 4
NCH = TILES // CH
FLOPS = 2 * B * K * (2 * NB)

PERM_V = ()
WARM_START = 0
WARM_EVERY = 0
WARM_CHUNKS = (0, 1)
PERM_G = {}
G_TILES = [15,19,22,26]
G_AT = {4:1,5:1, 6: 2}
G_SPLIT = 512
PRE = []
V_PRE = 0
S_PRE = 0
V_MID = 0
Y_ON_V = (3,)
V_UNITS = [2,4,4,4,3,3,3,3]
V_SPREAD = [0, 2, 3, 1, 4, 0]
S_UNITS = [3,4,3,4,3,4,4,4]
LOADS = ["V1a", "V1b", "L0", "V2", "G0", "L1", "G1a", "V3", "G1b", "L2", "G2a", "V4", "G2b", "L3", "G3a", "V5", "G3b", "L4", "G4a", "V6", "G4b", "L5", "G5a", "V7", "G5b", "L6", "G6", "L7", "G7a", "G7b"]


def tile_kktloss_pc_t_kernel(tc, Volt, Y_top, Yconj_top, PQ_Loads, PQ_Gens, out):
    nc = tc.nc
    with ExitStack() as ctx:
        ctx.enter_context(tc.manual_schedule())
        const = ctx.enter_context(tc.tile_pool(name="const", bufs=1))
        big = ctx.enter_context(tc.tile_pool(name="big", bufs=9))
        pqp = ctx.enter_context(tc.tile_pool(name="pqp", bufs=5))
        work = ctx.enter_context(tc.tile_pool(name="work", bufs=3))
        perm = ctx.enter_context(tc.tile_pool(name="perm", bufs=4))
        junk = ctx.enter_context(tc.tile_pool(name="junk", bufs=2))
        psum = ctx.enter_context(tc.psum_pool(name="psum", bufs=4))

        views = {
            "V": Volt.rearrange("(p t) k -> p t k", t=TILES),
            "L": PQ_Loads.rearrange("(p t) k -> p t k", t=TILES),
            "G": PQ_Gens.rearrange("(p t) k -> p t k", t=TILES),
        }
        held = {}

        def load(kind, n, lo, hi):
            if (kind, n) not in held:
                if kind == "V":
                    held[(kind, n)] = big.tile([P, CH, K], BF16, tag="v", name="v%d" % n)
                else:
                    held[(kind, n)] = pqp.tile([P, CH, K], BF16, tag="pq" + kind, name="pq%s%d" % (kind, n))
            nc.sync.dma_start(out=held[(kind, n)][:, lo:hi, :], in_=views[kind][:, n * CH + lo:n * CH + hi, :])

        def load_token(token):
            lo, hi = {"": (0, 4), "a": (0, 2), "b": (2, 4), "c": (0, 1), "d": (1, 2)}[token[2:]]
            load(token[0], int(token[1]), lo, hi)

        for token in PRE:
            load_token(token)
        y_raw = []
        for mat, src in enumerate((Y_top, Yconj_top)):
            raw = big.tile([P, CH, K], BF16, tag="v", name="yraw%d" % mat)
            for r in range(CH):
                nc.sync.dma_start(out=raw[:, r, :], in_=src[r * P:(r + 1) * P, :])
            y_raw.append(raw)
        for j in range(CH):
            load("V", 0, j, j + 1)
        for token in LOADS:
            load_token(token)

        ident = const.tile([P, P], F32)
        make_identity(nc, ident[:])
        y_codes = const.tile([P, 4 * NB], U32, align_bytes=64)
        y_scales = const.tile([P, 4 * NB], U8, align_bytes=64)
        sums = const.tile([P, TILES, 3], F32)
        if G_TILES:
            nc.vector.memset(sums[:, :, 1:2], 0.0)

        def permute(raw, j):
            pw = perm.tile([P, 2, 2, P], F32, tag="pw", name="pw")
            nc.vector.tensor_copy(out=pw[:], in_=raw[:, j, :].bitcast(F32).rearrange("p (g w u) -> p g u w", g=2, u=2))
            return pw

        def permute_g(raw, j):
            pw = perm.tile([P, 2, 2, P], F32, tag="pw", name="pwg")
            words = raw[:, j, :].rearrange("p (g w u e) -> p g u w e", g=2, u=2, e=2)
            for g in range(2):
                nc.gpsimd.tensor_scalar(out=pw[:, g, :, :].rearrange("p u w -> p (u w)").bitcast(BF16).rearrange("p (u w e) -> p u w e", u=2, e=2),
                                        in0=words[:, g], scalar1=1.0, scalar2=0.0, op0=ALU.mult, op1=ALU.add)
            return pw

        idle = const.tile([P, NB], BF16)
        nc.vector.memset(idle[:], 0.0)

        def transposes(raw, j, pw, tag, warm=0):
            tp = psum.tile([P, 4, P], F32, tag=tag, name="tp" + tag)
            for unused in range(warm):
                nc.tensor.matmul(out=tp[:].rearrange("p q b -> p (q b)"), lhsT=idle[:, 0:P], rhs=idle[:], start=True, stop=True)
            words = raw[:, j, :].bitcast(F32)
            for q in range(4):
                g, u = q // 2, q % 2
                if pw is not None:
                    src = pw[:, g, u, :]
                else:
                    src = words[:, g * 256 + u:(g + 1) * 256:2]
                nc.tensor.transpose(tp[:, q, :], src, ident[:])
            return tp

        units = []
        for token in PRE + LOADS:
            if token[0] != "V":
                n = int(token[1])
                lo, hi = {"": (0, 4), "a": (0, 2), "b": (2, 4), "c": (0, 1), "d": (1, 2)}[token[2:]]
                units.extend([(n * CH + j, "LG".index(token[0])) for j in range(lo, hi) if n * CH + j not in G_TILES])
        units.reverse()

        def d_vector():
            if units:
                t, w = units.pop()
                jv = junk.tile([P, K], BF16, tag="jv", name="jv")
                nc.vector.tensor_scalar(out=jv[:], in0=held[("LG"[w], t // CH)][:, t % CH, :], scalar1=(1.0 - 2.0 * w),
                                        scalar2=None, op0=ALU.mult, op1=ALU.add, accum_out=sums[:, t, w:w + 1])

        def d_scalar():
            if units:
                t, w = units.pop()
                js = junk.tile([P, K], BF16, tag="js", name="js")
                nc.scalar.activation(out=js[:], in_=held[("LG"[w], t // CH)][:, t % CH, :], func=ACT.Copy,
                                     scale=(1.0 - 2.0 * w), accum_out=sums[:, t, w:w + 1])

        for unused in range(V_PRE):
            d_vector()
        for unused in range(S_PRE):
            d_scalar()

        y_grp = []
        for mat in range(2):
            grp = work.tile([P, 4 * K], BF16, tag="grp", name="grpy", align_bytes=64)
            y_grp.append(grp)
            g32 = grp[:].bitcast(F32).rearrange("p (g i u) -> p g i u", g=2, u=2)
            for r in range(CH):
                warm = 1 if WARM_EVERY and r % WARM_EVERY == 0 else 0
                if mat == 0 and r == 0:
                    warm = WARM_START
                tp = transposes(y_raw[mat], r, None, ("tp", "acc")[mat], warm)
                src = tp[:].rearrange("p (g u) b -> p g b u", u=2)
                dst = g32[:, :, r * P:(r + 1) * P, :]
                if r in Y_ON_V:
                    nc.vector.tensor_copy(out=dst, in_=src)
                else:
                    nc.scalar.copy(out=dst, in_=src)

        def quantize_y(mat):
            for g in range(2):
                c0 = (mat * 2 + g) * NB
                nc.vector.quantize_mx(
                    out=y_codes[:, c0:c0 + NB].bitcast(FP8X4),
                    scales=y_scales[:, c0:c0 + NB],
                    in_=y_grp[mat][:, g * 4 * NB:(g + 1) * 4 * NB],
                )

        front = {}

        pws = {}

        def p_chunk(n):
            for j in PERM_G.get(n, ()):
                pws[(n, j)] = permute_g(held[("V", n)], j)

        def t_chunk(n):
            grp = work.tile([P, 4 * K], BF16, tag="grp", name="grpv", align_bytes=64)
            codes = work.tile([P, K], U32, tag="codes", name="codes", align_bytes=64)
            scales = work.tile([P, K], U8, tag="scales", name="scales", align_bytes=64)
            front[n] = (grp, codes, scales)
            for j in range(CH):
                pw = pws.pop((n, j)) if (n, j) in pws else None
                tp = transposes(held[("V", n)], j, pw, "tp", 1 if WARM_EVERY and n in WARM_CHUNKS and j % WARM_EVERY == 0 else 0)
                dst = grp[:, j * K:(j + 1) * K].bitcast(F32).rearrange("p (g b u) -> p g b u", g=2, u=2)
                nc.scalar.copy(out=dst, in_=tp[:].rearrange("p (g u) b -> p g b u", u=2))

        def q_chunk(n):
            grp, codes, scales = front[n]
            nc.vector.quantize_mx(out=codes[:].bitcast(FP8X4), scales=scales[:], in_=grp[:])

        accs = {}

        def m_chunk(n):
            grp, codes, scales = front[n]
            for j in range(CH):
                acc = psum.tile([P, NB], F32, tag="acc", name="acc")
                i = 0
                for g in range(2):
                    for mat in range(2):
                        c0 = j * 256 + g * P
                        y0 = (mat * 2 + g) * NB
                        nc.tensor.matmul_mx(
                            out=acc[:],
                            lhsT=codes[:, c0:c0 + P].bitcast(FP8X4),
                            lhsT_scale=scales[:, c0:c0 + P],
                            rhs=y_codes[:, y0:y0 + NB].bitcast(FP8X4),
                            rhs_scale=y_scales[:, y0:y0 + NB],
                            start=(i == 0),
                            stop=(i == 3),
                        )
                        i += 1
                accs[n * CH + j] = acc

        def c_tile(t):
            je = junk.tile([P, NB], F32, tag="je", name="je")
            nc.vector.scalar_tensor_tensor(
                out=je[:], in0=accs[t][:], scalar=1.0, in1=held[("V", t // CH)][:, t % CH, 0:NB],
                op0=ALU.mult, op1=ALU.mult, accum_out=sums[:, t, 2:3],
            )

        g_acc = const.tile([P, max(len(G_TILES), 1), P], F32)
        g_left = list(G_TILES)

        def g_tile():
            if not g_left:
                return
            t = g_left.pop(0)
            slot = G_TILES.index(t)
            pl, pg = held[("L", t // CH)][:, t % CH, :], held[("G", t // CH)][:, t % CH, :]
            gd = junk.tile([P, K], F32, tag="gd", name="gd")
            for c in range(0, K, G_SPLIT):
                nc.gpsimd.tensor_tensor(out=gd[:, c:c + G_SPLIT], in0=pl[:, c:c + G_SPLIT], in1=pg[:, c:c + G_SPLIT], op=ALU.subtract)
            width = K // 2
            while width > P:
                for c in range(0, width, G_SPLIT):
                    step = min(G_SPLIT, width)
                    nc.gpsimd.tensor_tensor(out=gd[:, c:c + step], in0=gd[:, c:c + step], in1=gd[:, width + c:width + c + step], op=ALU.add)
                width //= 2
            nc.gpsimd.tensor_tensor(out=g_acc[:, slot, :], in0=gd[:, 0:P], in1=gd[:, P:2 * P], op=ALU.add)

        quantize_y(0)
        for unused in range(V_MID):
            d_vector()
        t_chunk(0)
        quantize_y(1)
        q_chunk(0)
        for n in range(NCH):
            more = n + 1 < NCH
            if more:
                t_chunk(n + 1)
            if n + 2 < NCH:
                p_chunk(n + 2)
            m_chunk(n)
            s_left = S_UNITS[n]
            for unused in range(G_AT.get(n, 0)):
                g_tile()
            slots = [0, 0, 0, 0, 0]
            for i in range(V_UNITS[n]):
                slots[V_SPREAD[i % 6]] += 1
            plan = ["d"] * slots[0] + ["q"] + ["d"] * slots[1] + [0] + ["d"] * slots[2] + [1] + ["d"] * slots[3] + [2] + ["d"] * slots[4] + [3]
            for step in plan:
                if step == "d":
                    d_vector()
                    if s_left:
                        s_left -= 1
                        d_scalar()
                elif step == "q":
                    if more:
                        q_chunk(n + 1)
                else:
                    c_tile(n * CH + step)
            for unused in range(s_left):
                d_scalar()
        for slot, t in enumerate(G_TILES):
            nc.vector.tensor_reduce(out=sums[:, t, 0:1], in_=g_acc[:, slot, :], axis=AX.X, op=ALU.add)
        turn = 0
        while units:
            if turn % 2 == 0:
                d_scalar()
            else:
                d_vector()
            turn += 1
        res = const.tile([P, TILES], F32)
        nc.vector.tensor_reduce(out=res[:], in_=sums[:], axis=AX.X, op=ALU.add)
        nc.sync.dma_start(out=out.rearrange("(p t) -> p t", t=TILES), in_=res[:])
